import numpy as np
import ml_dtypes


def mxq(x, axis, fmt="e4m3"):
    dtype, down = {"e4m3": (ml_dtypes.float8_e4m3fn, 7), "e5m2": (ml_dtypes.float8_e5m2, 14)}[fmt]
    v = np.moveaxis(np.asarray(x, np.float32).astype(ml_dtypes.bfloat16).astype(np.float64), axis, -1)
    blocks = v.reshape(v.shape[:-1] + (-1, 32))
    amax = np.abs(blocks).max(-1, keepdims=True)
    byte = np.maximum(np.where(amax > 0, np.frexp(amax)[1] - 1 + 127, 0) - down, 1)
    scale = np.exp2(byte - 127.0)
    codes = (blocks / scale).astype(np.float32).astype(dtype).astype(np.float64)
    return np.moveaxis((codes * scale).reshape(v.shape), -1, axis)


WIDE = False


def mx_kscale(k):
    if not WIDE:
        return np.ones(k)
    levels = np.array([18, -18])
    if k % 512:
        return np.exp2(np.random.permutation(np.resize(levels, k // 32))).repeat(32)
    a = np.empty((k // 512, 16))
    for p in range(k // 512):
        a[p, :8] = np.random.permutation(np.resize(levels, 8))
        for g in range(8):
            far = levels[np.abs(levels - a[p, g]) >= 10]
            a[p, g + 8] = far[np.random.randint(len(far))]
    return np.exp2(a.ravel()).repeat(32)


BF16 = ml_dtypes.bfloat16


def bf(x):
    return np.asarray(x, np.float32).astype(BF16)


def f64(x):
    return np.asarray(x).astype(np.float64)


N, DHID, DOUT, NF = 1024, 1024, 512, 32
G = 3 * DHID
FS = N // NF
SYNC = 0.15


def sigmoid(v):
    return 1.0 / (1.0 + np.exp(-v))


def setup_inputs():
    s = mx_kscale(N)
    u = mx_kscale(DHID)
    o = np.random.standard_normal((N, DOUT)) * (0.8 + 0.8 * np.random.random((N, 1)))
    rows = np.concatenate([np.full(DOUT, 0.55 / np.sqrt(DOUT)), np.array([0.3])])
    eng0 = bf(o)
    ten0 = bf((o * o).mean(-1))
    hiddens = bf(np.random.standard_normal((N, DHID)) * (0.5 + np.random.random((N, 1))))
    w_ih0 = bf(np.random.standard_normal((DOUT + 1, G)) * rows[:, None])
    b_ih = bf(np.random.standard_normal(G) * 0.3)
    w_hh = bf(np.random.standard_normal((DHID, G)) * 0.7 / np.sqrt(DHID))
    b_hh = bf(np.random.standard_normal(G) * 0.3)
    wi = f64(w_ih0)
    gi = f64(eng0) @ wi[:DOUT] + f64(ten0)[:, None] * wi[DOUT] + f64(b_ih)
    gh = f64(hiddens) @ f64(w_hh) + f64(b_hh)
    rz = sigmoid(gi[:, :2 * DHID] + gh[:, :2 * DHID])
    hn = gh[:, 2 * DHID:]
    ncand = np.tanh(gi[:, 2 * DHID:] + rz[:, :DHID] * hn)
    g = np.random.standard_normal((N, DHID)) * np.exp2(np.random.randint(-6, 1, (N, 1))) * 8.0
    return {
        "eng_out": bf(f64(eng0) * s[:, None]),
        "tension": bf(f64(ten0) * s),
        "hiddens": hiddens,
        "w_ih": bf(f64(w_ih0) / np.concatenate([u, u, u])),
        "b_ih": b_ih,
        "w_hh": w_hh,
        "b_hh": b_hh,
        "rz": np.asarray(rz, np.float32),
        "ncand": np.asarray(ncand, np.float32),
        "hn": np.asarray(hn, np.float32),
        "grad_out": bf(g / s[:, None] * u),
    }


def reference(eng_out, tension, hiddens, w_ih, b_ih, w_hh, b_hh, rz, ncand, hn, grad_out):
    g = f64(grad_out)
    h = f64(hiddens)
    n = f64(ncand)
    r, z = np.split(f64(rz), 2, axis=-1)
    gf = g.reshape(NF, FS, DHID)
    dh = ((1.0 - SYNC) * gf + SYNC * gf.mean(axis=1, keepdims=True)).reshape(N, DHID)
    dn = dh * (1.0 - z) * (1.0 - n * n)
    dzg = dh * (h - n) * z * (1.0 - z)
    dr = dn * f64(hn) * r * (1.0 - r)
    dgi = np.concatenate([dr, dzg, dn], axis=-1)
    deng = mxq(dgi, 1, "e5m2") @ mxq(f64(w_ih)[:DOUT], 1, "e4m3").T
    dw = mxq(f64(eng_out), 0, "e4m3").T @ mxq(dgi, 0, "e5m2")
    dlast = (f64(tension)[:, None] * dgi).sum(axis=0, keepdims=True)
    return deng, np.concatenate([dw, dlast], axis=0)

@@ -1,0 +1,565 @@
+from contextlib import ExitStack
+
+import concourse.mybir as mybir
+from concourse.masks import make_block_diagonal, make_identity
+
+N, DHID, DOUT = 1024, 1024, 512
+FACTION = 32
+SYNC = 0.15
+FLOPS = 2 * 2 * N * 3 * DHID * DOUT
+BYTES = (N * DOUT + N + 2 * N * DHID + DOUT * 3 * DHID) * 2 + 4 * N * DHID * 4 + (N * DOUT + (DOUT + 1) * 3 * DHID) * 4
+
+F32 = mybir.dt.float32
+BF16 = mybir.dt.bfloat16
+U32 = mybir.dt.uint32
+U8 = mybir.dt.uint8
+E4M3 = mybir.dt.float8_e4m3fn_x4
+E5M2 = mybir.dt.float8_e5m2_x4
+ALU = mybir.AluOpType
+ACT = mybir.ActivationFunctionType
+
+P = 128
+PACK = 4
+W = P * PACK
+UNIT = PACK * W
+MEAN_SHARE = SYNC / FACTION
+OWN_OVER_MEAN = (1.0 - SYNC) / MEAN_SHARE
+GATE_R, GATE_Z, GATE_N = 0, 1, 2
+LAST_WIDE = 40
+UNITS = [(0, 0), (0, 1), (1, 0), (1, 1)]
+
+
+def tile_fractalengine_pb_v_kernel(
+    tc, eng_out, tension, hiddens, w_ih, b_ih, w_hh, b_hh, rz, ncand, hn, grad_out, out_0, out_1
+):
+    nc = tc.nc
+    with ExitStack() as ctx:
+        keep = ctx.enter_context(tc.tile_pool(name="keep", bufs=1))
+        work = ctx.enter_context(tc.tile_pool(name="work", bufs=2))
+        psum = ctx.enter_context(tc.psum_pool(name="psum", bufs=1))
+
+        ident = keep.tile([P, P], F32, name="ident")
+        make_identity(nc, ident[:])
+        same_f32 = keep.tile([P, P], F32, name="same_f32")
+        make_block_diagonal(nc, same_f32[:], FACTION // PACK)
+        last_cols = keep.tile([P, P], F32, name="last_cols")
+        nc.gpsimd.memset(last_cols[:], 0.0)
+
+        ctx.enter_context(tc.manual_schedule(engines={mybir.EngineType.SP}))
+
+        same_faction = keep.tile([P, P], BF16, name="same_faction")
+        nc.scalar.activation(out=same_faction[:], in_=same_f32[:], func=ACT.Square)
+
+        sources = {
+            "n": (ncand, 0, F32),
+            "h": (hiddens, 0, BF16),
+            "g": (grad_out, 0, BF16),
+            "z": (rz, DHID, F32),
+            "r": (rz, 0, F32),
+            "hn": (hn, 0, F32),
+        }
+        tiles = {}
+
+        def bank(b, name):
+            return psum.tile([P, W], F32, name=name, tag="bank%d" % b)
+
+        def by_slot(ap):
+            return ap.rearrange("p (j f) -> p j f", f=W)
+
+        def load(name, u, half=None):
+            c, g = UNITS[u]
+            src, col0, dtype = sources[name]
+            if (name, u) not in tiles:
+                tiles[name, u] = work.tile([P, UNIT], dtype, name="in_" + name, tag="in_" + name)
+            rows = src[g * W : (g + 1) * W, col0 + c * W : col0 + (c + 1) * W].rearrange("(p j) f -> p j f", j=PACK)
+            j0, j1 = (0, PACK) if half is None else (2 * half, 2 * half + 2)
+            nc.sync.dma_start(out=by_slot(tiles[name, u][:, j0 * W : j1 * W]), in_=rows[:, j0:j1, :])
+
+        def part(name, u, half):
+            j0, j1 = (0, PACK) if half is None else (2 * half, 2 * half + 2)
+            return tiles[name, u][:, j0 * W : j1 * W]
+
+        def fresh(name, u, bufs):
+            if (name, u) not in tiles:
+                tiles[name, u] = work.tile([P, UNIT], F32, name=name, tag=name, bufs=bufs)
+
+        def faction_sums(u):
+            tiles["sums", u] = bank(3, "sums")
+            for j in range(PACK):
+                nc.tensor.matmul(
+                    out=tiles["sums", u][:], lhsT=same_faction[:], rhs=tiles["g", u][:, j * W : (j + 1) * W],
+                    start=(j == 0), stop=(j == PACK - 1),
+                )
+
+        def n_minus_h(u, half=None):
+            fresh("dz", u, 2)
+            nc.vector.tensor_tensor(out=part("dz", u, half), in0=part("n", u, half), in1=part("h", u, half), op=ALU.subtract)
+
+        def pull_back(u, half=None):
+            fresh("a", u, 1)
+            slots = PACK if half is None else 2
+            nc.vector.scalar_tensor_tensor(
+                out=by_slot(part("a", u, half)), in0=by_slot(part("g", u, half)), scalar=OWN_OVER_MEAN,
+                in1=tiles["sums", u][:].unsqueeze(1).to_broadcast([P, slots, W]), op0=ALU.mult, op1=ALU.add,
+            )
+
+        def through_z(u, half=None):
+            nc.vector.scalar_tensor_tensor(
+                out=part("a", u, half), in0=part("z", u, half), scalar=1.0, in1=part("a", u, half),
+                op0=ALU.subtract, op1=ALU.mult,
+            )
+
+        def square_n(u, half=None):
+            nc.scalar.activation(out=part("n", u, half), in_=part("n", u, half), func=ACT.Square)
+
+        def finish_dn(u, half=None):
+            nc.vector.scalar_tensor_tensor(
+                out=part("n", u, half), in0=part("n", u, half), scalar=1.0, in1=part("a", u, half),
+                op0=ALU.subtract, op1=ALU.mult,
+            )
+
+        def times_z(u, half=None):
+            nc.vector.tensor_tensor(out=part("dz", u, half), in0=part("dz", u, half), in1=part("z", u, half), op=ALU.mult)
+
+        def finish_dz(u):
+            nc.vector.scalar_tensor_tensor(
+                out=part("dz", u, None), in0=part("dz", u, None), scalar=MEAN_SHARE, in1=part("a", u, None),
+                op0=ALU.mult, op1=ALU.mult,
+            )
+
+        def square_r(u, half=None):
+            nc.scalar.activation(out=part("r", u, half), in_=part("r", u, half), func=ACT.Square, bias=-0.5)
+
+        def times_hn(u):
+            nc.vector.scalar_tensor_tensor(
+                out=part("r", u, None), in0=part("r", u, None), scalar=0.25, in1=part("hn", u, None),
+                op0=ALU.subtract, op1=ALU.mult,
+            )
+
+        def finish_dr(u):
+            nc.vector.scalar_tensor_tensor(
+                out=part("r", u, None), in0=part("r", u, None), scalar=-MEAN_SHARE, in1=part("n", u, None),
+                op0=ALU.mult, op1=ALU.mult,
+            )
+
+        holder = {GATE_R: "r", GATE_Z: "dz", GATE_N: "n"}
+
+        ten_raw = keep.tile([P, 2, PACK], BF16, name="ten_raw")
+        ten = keep.tile([P, 2 * PACK, LAST_WIDE], F32, name="ten")
+        ten_n = keep.tile([P, 2 * PACK, LAST_WIDE], F32, name="ten_n")
+
+        def load_tension():
+            nc.sync.dma_start(out=ten_raw[:], in_=tension.rearrange("(g p j) -> p g j", p=P, j=PACK))
+
+        def widen_tension():
+            wide = ten_raw[:].rearrange("p g j -> p (g j)").unsqueeze(2).to_broadcast([P, 2 * PACK, LAST_WIDE])
+            nc.scalar.activation(out=ten[:], in_=wide, func=ACT.Copy)
+            nc.scalar.activation(out=ten_n[:], in_=wide, func=ACT.Copy, scale=MEAN_SHARE)
+
+        def last_row_sums(gate, u, fbs=range(PACK)):
+            c, g = UNITS[u]
+            weights = ten_n if gate == GATE_N else ten
+            for fb in fbs:
+                if gate == GATE_N and fb == 0 and g == 0:
+                    tiles["last", c] = bank(0, "last_acc")
+                col = (gate * PACK + fb) * LAST_WIDE
+                for j in range(PACK):
+                    nc.tensor.matmul(
+                        out=tiles["last", c][:, col : col + LAST_WIDE],
+                        lhsT=tiles[holder[gate], u][:, j * W + fb * P : j * W + (fb + 1) * P],
+                        rhs=weights[:, g * PACK + j, :],
+                        start=(g == 0 and gate == GATE_N and fb == 0 and j == 0),
+                        stop=(g == 1 and gate == GATE_R and fb == PACK - 1 and j == PACK - 1),
+                    )
+
+        def empty_last_row(c):
+            nc.scalar.copy(
+                out=last_cols[:, : 6 * PACK].rearrange("p (gate c fb) -> p gate c fb", c=2, fb=PACK)[:, :, c, :],
+                in_=tiles["last", c][:, : 3 * PACK * LAST_WIDE].rearrange("p (gate fb n) -> p gate fb n", fb=PACK, n=LAST_WIDE)[:, :, :, 0],
+            )
+
+        def store_last_row():
+            blocks = 3 * DHID // P
+            turned = bank(0, "last_turned")
+            nc.tensor.transpose(turned[:, :P], last_cols[:], ident[:])
+            last_rows = keep.tile([32, P], F32, name="last_rows")
+            nc.scalar.copy(out=last_rows[:], in_=turned[:32, :P])
+            nc.sync.dma_start(
+                out=out_1[DOUT : DOUT + 1, :].rearrange("o (b f) -> (o b) f", f=P), in_=last_rows[:blocks, :]
+            )
+
+        def round_tokens(gate, u, on_vector=False, m0=0, m1=P):
+            if ("tok", gate, u) not in tiles:
+                tiles["tok", gate, u] = work.tile([P, UNIT], BF16, name="tok", tag="tok", bufs=3, align_bytes=64)
+            src = tiles[holder[gate], u][:].rearrange("p (j m t) -> p m j t", j=PACK, t=PACK)[:, m0:m1]
+            dst = tiles["tok", gate, u][:].rearrange("p (t m j) -> p m j t", j=PACK, t=PACK)[:, m0:m1]
+            if gate == GATE_N:
+                nc.scalar.activation(out=dst, in_=src, func=ACT.Copy, scale=MEAN_SHARE)
+            elif on_vector:
+                nc.vector.tensor_copy(out=dst, in_=src)
+            else:
+                nc.scalar.copy(out=dst, in_=src)
+
+        def quantise(key, src, fmt, tag, bufs, half=None):
+            if ("codes",) + key not in tiles:
+                tiles[("codes",) + key] = work.tile([P, W], U32, name="codes_" + tag, tag="codes_" + tag, bufs=bufs, align_bytes=64)
+                tiles[("scales",) + key] = work.tile([P, W], U8, name="scales_" + tag, tag="scales_" + tag, bufs=bufs, align_bytes=64)
+            c0, c1 = (0, W) if half is None else (half * W // 2, (half + 1) * W // 2)
+            nc.vector.quantize_mx(
+                out=tiles[("codes",) + key][:, c0:c1].bitcast(fmt), scales=tiles[("scales",) + key][:, c0:c1],
+                in_=src[:, c0 * PACK : c1 * PACK],
+            )
+
+        def quantise_tokens(gate, u):
+            quantise(("tok", gate, u), tiles["tok", gate, u], E5M2, "tok", 9)
+
+        def turn(gate, u, jjs=(0, 1)):
+            words = tiles["tok", gate, u][:].bitcast(F32)
+            for jj in jjs:
+                tiles["turned", gate, u, jj] = bank(1 + jj, "turned")
+                for t in range(PACK):
+                    nc.tensor.transpose(
+                        tiles["turned", gate, u, jj][:, t * P : (t + 1) * P],
+                        words[:, 2 * P * t + jj : 2 * P * (t + 1) : 2], ident[:],
+                    )
+
+        def group_features(gate, u, jj, on_vector=False):
+            if jj == 0:
+                tiles["feat", gate, u] = work.tile([P, UNIT], BF16, name="feat", tag="feat", bufs=3, align_bytes=64)
+            move = nc.vector.tensor_copy if on_vector else nc.scalar.copy
+            move(
+                out=tiles["feat", gate, u][:, jj * 2 * W : (jj + 1) * 2 * W].rearrange("q (e p t) -> q e p t", e=2, t=PACK),
+                in_=tiles["turned", gate, u, jj][:].bitcast(BF16).rearrange("q (t p e) -> q e p t", e=2, t=PACK),
+            )
+
+        def group_both(gate, u):
+            group_features(gate, u, 0)
+            group_features(gate, u, 1)
+
+        def quantise_features(gate, u, half=None):
+            quantise(("feat", gate, u), tiles["feat", gate, u], E5M2, "kept" if u == 1 else "feat", 3, half)
+
+        def load_eng(g):
+            tiles["eng_raw", g] = work.tile([P, UNIT], BF16, name="raw", tag="raw", bufs=3)
+            nc.sync.dma_start(
+                out=by_slot(tiles["eng_raw", g][:]),
+                in_=eng_out[g * W : (g + 1) * W, :].rearrange("(p j) d -> p j d", j=PACK),
+            )
+
+        def group_eng(g):
+            tiles["eng", g] = work.tile([P, UNIT], BF16, name="side", tag="side", bufs=2, align_bytes=64)
+            nc.scalar.copy(
+                out=tiles["eng", g][:].rearrange("p (c i j) -> p c j i", i=PACK, j=PACK),
+                in_=tiles["eng_raw", g][:].rearrange("p (j c i) -> p c j i", i=PACK, j=PACK),
+            )
+
+        def quantise_eng(g):
+            quantise(("eng", g), tiles["eng", g], E4M3, "eng", 2)
+
+        def load_w(gate, c):
+            tiles["w_raw", gate, c] = work.tile([P, UNIT], BF16, name="raw", tag="raw", bufs=3)
+            col0 = gate * DHID + c * W
+            nc.sync.dma_start(
+                out=by_slot(tiles["w_raw", gate, c][:]),
+                in_=w_ih[:DOUT, col0 : col0 + W].rearrange("(dt p) f -> p dt f", p=P),
+            )
+
+        def turn_w(gate, c):
+            words = tiles["w_raw", gate, c][:].bitcast(F32)
+            for pair in range(2):
+                tiles["w_turned", gate, c, pair] = bank(1 + pair, "w_turned")
+                for k in range(PACK):
+                    dt = 2 * pair + k // 2
+                    nc.tensor.transpose(
+                        tiles["w_turned", gate, c, pair][:, k * P : (k + 1) * P],
+                        words[:, 2 * P * dt + k % 2 : 2 * P * (dt + 1) : 2], ident[:],
+                    )
+
+        def group_w(gate, c):
+            tiles["w", gate, c] = work.tile([P, UNIT], BF16, name="side", tag="side", bufs=2, align_bytes=64)
+            for pair in range(2):
+                nc.scalar.copy(
+                    out=tiles["w", gate, c][:, pair * 2 * W : (pair + 1) * 2 * W].bitcast(F32).rearrange("q (d r v) -> q d r v", d=2, v=2),
+                    in_=tiles["w_turned", gate, c, pair][:].rearrange("q (d v r) -> q d r v", d=2, v=2),
+                )
+
+        def quantise_w(gate, c):
+            quantise(("w", gate, c), tiles["w", gate, c], E4M3, "w", 6)
+
+        def staging(key):
+            if key not in tiles:
+                tiles[key] = work.tile([P, UNIT], F32, name="staging", tag="staging", bufs=3)
+            return tiles[key]
+
+        def weight_grad(gate, c, dt, b):
+            acc = bank(b, "dw")
+            tiles["dw", gate, c, dt] = acc
+            for g in range(2):
+                u = UNITS.index((c, g))
+                nc.tensor.matmul_mx(
+                    out=acc[:],
+                    lhsT=tiles["codes", "eng", g][:, dt * P : (dt + 1) * P].bitcast(E4M3),
+                    lhsT_scale=tiles["scales", "eng", g][:, dt * P : (dt + 1) * P],
+                    rhs=tiles["codes", "tok", gate, u][:].bitcast(E5M2),
+                    rhs_scale=tiles["scales", "tok", gate, u][:],
+                    start=(g == 0), stop=(g == 1),
+                )
+
+        def empty_weight_grad(gate, c, dt, on_vector=False):
+            dst = staging(("dw_out", gate, c))[:, dt * W : (dt + 1) * W].rearrange("p (m t) -> p m t", t=PACK)
+            src = tiles["dw", gate, c, dt][:].rearrange("p (t m) -> p m t", t=PACK)
+            if on_vector:
+                nc.vector.tensor_copy(out=dst, in_=src)
+            else:
+                nc.scalar.copy(out=dst, in_=src)
+
+        def store_weight_grad(gate, c, dts):
+            col0 = gate * DHID + c * W
+            nc.sync.dma_start(
+                out=out_1[:DOUT, col0 : col0 + W].rearrange("(dt p) f -> p dt f", p=P)[:, dts, :],
+                in_=by_slot(tiles["dw_out", gate, c][:])[:, dts, :],
+            )
+
+        def input_grad(g, j, gate, c, b=None):
+            if b is not None:
+                tiles["dx", g, j] = bank(b, "dx")
+            u = UNITS.index((c, g))
+            nc.tensor.matmul_mx(
+                out=tiles["dx", g, j][:],
+                lhsT=tiles["codes", "feat", gate, u][:, j * P : (j + 1) * P].bitcast(E5M2),
+                lhsT_scale=tiles["scales", "feat", gate, u][:, j * P : (j + 1) * P],
+                rhs=tiles["codes", "w", gate, c][:].bitcast(E4M3),
+                rhs_scale=tiles["scales", "w", gate, c][:],
+                start=(b is not None), stop=(gate == GATE_R and c == 1),
+            )
+
+        def empty_input_grad(g, j, on_vector=False):
+            dst = staging(("dx_out", g))[:, j * W : (j + 1) * W]
+            if on_vector:
+                nc.vector.tensor_copy(out=dst, in_=tiles["dx", g, j][:])
+            else:
+                nc.scalar.copy(out=dst, in_=tiles["dx", g, j][:])
+
+        def store_input_grad(g, js):
+            nc.sync.dma_start(
+                out=out_0[g * W : (g + 1) * W, :].rearrange("(p j) d -> p j d", j=PACK)[:, js, :],
+                in_=by_slot(tiles["dx_out", g][:])[:, js, :],
+            )
+
+        def input_passes(gate, u, js=range(PACK)):
+            c, g = UNITS[u]
+            for j in js:
+                input_grad(g, j, gate, c, 4 + j if (gate == GATE_N and c == 0) else None)
+
+        waiting = []
+        filled = []
+
+        def next_dw(refill=True, b=3, on_vector=False):
+            if filled:
+                gate, c, dt = filled.pop()
+                empty_weight_grad(gate, c, dt, on_vector)
+                if dt == PACK - 1:
+                    store_weight_grad(gate, c, slice(0, PACK))
+            if refill and waiting:
+                gate, c, dt = waiting.pop(0)
+                weight_grad(gate, c, dt, b)
+                filled.append((gate, c, dt))
+
+        def queue_dw(gate, u):
+            c, g = UNITS[u]
+            if g == 1:
+                waiting.extend([(gate, c, dt) for dt in range(PACK)])
+
+        def w_pass(gate, c):
+            turn_w(gate, c)
+            group_w(gate, c)
+
+        def round_shared(gate, u, split):
+            round_tokens(gate, u, True, 0, split)
+            round_tokens(gate, u, False, split, P)
+
+        load("g", 0)
+        load("n", 0, 0)
+        load("h", 0, 0)
+        load("z", 0, 0)
+        load("n", 0, 1)
+        load("h", 0, 1)
+        load("z", 0, 1)
+        load_w(GATE_N, 0)
+        load_tension()
+        load("r", 0)
+        load_eng(0)
+        load("hn", 0)
+        load_w(GATE_Z, 0)
+        faction_sums(0)
+        n_minus_h(0, 0)
+        square_n(0, 0)
+        pull_back(0, 0)
+        pull_back(0, 1)
+        through_z(0, 0)
+        n_minus_h(0, 1)
+        square_n(0, 1)
+        through_z(0, 1)
+        widen_tension()
+        w_pass(GATE_N, 0)
+        for name in ("g", "n", "h", "z"):
+            load(name, 1)
+        load_w(GATE_R, 0)
+        load("r", 1)
+        load("hn", 1)
+        finish_dn(0, 0)
+        square_r(0)
+        finish_dn(0, 1)
+
+        for u in range(len(UNITS)):
+            c, g = UNITS[u]
+            last = u == len(UNITS) - 1
+            if u > 0:
+                n_minus_h(u)
+                last_row_sums(GATE_R, u - 1, range(2))
+                quantise_features(GATE_Z, u - 1)
+                square_n(u)
+                turn(GATE_R, u - 1)
+                if g == 1:
+                    input_passes(GATE_Z, u - 1)
+                pull_back(u)
+                quantise_tokens(GATE_R, u - 1)
+                last_row_sums(GATE_R, u - 1, range(2, 4))
+                queue_dw(GATE_Z, u - 1)
+                queue_dw(GATE_R, u - 1)
+                next_dw()
+                if not last:
+                    for name in ("g", "n", "h", "z", "r", "hn"):
+                        load(name, u + 1)
+                group_features(GATE_R, u - 1, 0)
+                next_dw()
+                group_features(GATE_R, u - 1, 1)
+                next_dw()
+                through_z(u)
+                square_r(u, 0)
+                next_dw()
+                square_r(u, 1)
+                next_dw()
+                quantise_features(GATE_R, u - 1)
+                if g == 1:
+                    input_passes(GATE_R, u - 1)
+                finish_dn(u)
+                if u == 1:
+                    group_eng(1)
+                    load_w(GATE_Z, 1)
+                if u == 2:
+                    empty_last_row(0)
+                    next_dw()
+                if u == 3:
+                    for j in range(PACK):
+                        empty_input_grad(0, j)
+                    store_input_grad(0, slice(0, PACK))
+            last_row_sums(GATE_N, u, range(2))
+            round_tokens(GATE_N, u, False, 0, P // 2)
+            next_dw()
+            last_row_sums(GATE_N, u, range(2, 4))
+            round_tokens(GATE_N, u, False, P // 2, P)
+            next_dw()
+            times_z(u)
+            turn(GATE_N, u)
+            if u == 0:
+                quantise_w(GATE_N, 0)
+                group_eng(0)
+                load_eng(1)
+            if u == 1:
+                quantise_eng(1)
+            if u == 3:
+                input_passes(GATE_N, 1)
+                input_passes(GATE_Z, 1)
+            next_dw()
+            if not last:
+                times_hn(u)
+            quantise_tokens(GATE_N, u)
+            queue_dw(GATE_N, u)
+            next_dw()
+            group_features(GATE_N, u, 0)
+            next_dw()
+            group_features(GATE_N, u, 1)
+            next_dw()
+            finish_dz(u)
+            if last:
+                times_hn(u)
+                input_passes(GATE_R, 1)
+            if u == 0:
+                quantise_eng(0)
+                w_pass(GATE_Z, 0)
+                load_w(GATE_N, 1)
+            if u == 2:
+                w_pass(GATE_Z, 1)
+            last_row_sums(GATE_Z, u, range(2))
+            next_dw()
+            if last:
+                round_tokens(GATE_Z, u, True)
+                quantise_features(GATE_N, u)
+                next_dw()
+                turn(GATE_Z, u)
+                input_passes(GATE_N, u)
+                quantise_tokens(GATE_Z, u)
+                last_row_sums(GATE_Z, u, range(2, 4))
+                finish_dr(u)
+            else:
+                quantise_features(GATE_N, u)
+                round_shared(GATE_Z, u, P // 2)
+                next_dw(refill=False)
+                last_row_sums(GATE_Z, u, range(2, 4))
+                if u == 0:
+                    quantise_w(GATE_Z, 0)
+                    w_pass(GATE_R, 0)
+                if u == 1:
+                    w_pass(GATE_N, 1)
+                    load_w(GATE_R, 1)
+                if u == 2:
+                    quantise_w(GATE_Z, 1)
+                    w_pass(GATE_R, 1)
+                finish_dr(u)
+                turn(GATE_Z, u)
+                if g == 0:
+                    input_passes(GATE_N, u)
+                faction_sums(u + 1)
+                quantise_tokens(GATE_Z, u)
+                quantise_w(GATE_N if u == 1 else GATE_R, 1 if u > 0 else 0)
+                group_both(GATE_Z, u)
+                round_tokens(GATE_R, u)
+
+        u = len(UNITS) - 1
+        queue_dw(GATE_Z, u)
+        next_dw()
+        group_features(GATE_Z, u, 0)
+        next_dw()
+        group_features(GATE_Z, u, 1)
+        next_dw()
+        round_shared(GATE_R, u, 96)
+        quantise_features(GATE_Z, u)
+        next_dw()
+        turn(GATE_R, u)
+        quantise_tokens(GATE_R, u)
+        next_dw()
+        input_passes(GATE_Z, u)
+        weight_grad(GATE_R, 1, 0, 3)
+        group_features(GATE_R, u, 0)
+        group_features(GATE_R, u, 1, on_vector=True)
+        weight_grad(GATE_R, 1, 1, 1)
+        empty_weight_grad(GATE_R, 1, 0)
+        quantise_features(GATE_R, u)
+        weight_grad(GATE_R, 1, 2, 2)
+        input_passes(GATE_R, u)
+        weight_grad(GATE_R, 1, 3, 3)
+        last_row_sums(GATE_R, u)
+        empty_weight_grad(GATE_R, 1, 1)
+        store_weight_grad(GATE_R, 1, slice(0, 2))
+        empty_weight_grad(GATE_R, 1, 2, on_vector=True)
+        empty_input_grad(1, 0)
+        empty_input_grad(1, 1, on_vector=True)
+        store_input_grad(1, slice(0, 2))
+        empty_input_grad(1, 2)
+        empty_input_grad(1, 3, on_vector=True)
+        store_input_grad(1, slice(2, 4))
+        empty_weight_grad(GATE_R, 1, 3)
+        store_weight_grad(GATE_R, 1, slice(2, 4))
+        empty_last_row(1)
+        store_last_row()

@@ -26,7 +26,9 @@ MEAN_SHARE = SYNC / FACTION
 OWN_OVER_MEAN = (1.0 - SYNC) / MEAN_SHARE
 GATE_R, GATE_Z, GATE_N = 0, 1, 2
 LAST_WIDE = 40
-UNITS = [(0, 0), (0, 1), (1, 0), (1, 1)]
+R_SPLIT = 64
+TAIL_SPLIT = 88
+UNITS = [(0, 0), (0, 1), (1, 1), (1, 0)]
 
 
 def tile_fractalengine_pb_v_kernel(
@@ -45,7 +47,7 @@ def tile_fractalengine_pb_v_kernel(
         last_cols = keep.tile([P, P], F32, name="last_cols")
         nc.gpsimd.memset(last_cols[:], 0.0)
 
-        ctx.enter_context(tc.manual_schedule(engines={mybir.EngineType.SP}))
+        ctx.enter_context(tc.manual_schedule())
 
         same_faction = keep.tile([P, P], BF16, name="same_faction")
         nc.scalar.activation(out=same_faction[:], in_=same_f32[:], func=ACT.Square)
@@ -160,7 +162,7 @@ def tile_fractalengine_pb_v_kernel(
             c, g = UNITS[u]
             weights = ten_n if gate == GATE_N else ten
             for fb in fbs:
-                if gate == GATE_N and fb == 0 and g == 0:
+                if gate == GATE_N and fb == 0 and u % 2 == 0:
                     tiles["last", c] = bank(0, "last_acc")
                 col = (gate * PACK + fb) * LAST_WIDE
                 for j in range(PACK):
@@ -168,8 +170,8 @@ def tile_fractalengine_pb_v_kernel(
                         out=tiles["last", c][:, col : col + LAST_WIDE],
                         lhsT=tiles[holder[gate], u][:, j * W + fb * P : j * W + (fb + 1) * P],
                         rhs=weights[:, g * PACK + j, :],
-                        start=(g == 0 and gate == GATE_N and fb == 0 and j == 0),
-                        stop=(g == 1 and gate == GATE_R and fb == PACK - 1 and j == PACK - 1),
+                        start=(u % 2 == 0 and gate == GATE_N and fb == 0 and j == 0),
+                        stop=(u % 2 == 1 and gate == GATE_R and fb == PACK - 1 and j == PACK - 1),
                     )
 
         def empty_last_row(c):
@@ -193,7 +195,9 @@ def tile_fractalengine_pb_v_kernel(
                 tiles["tok", gate, u] = work.tile([P, UNIT], BF16, name="tok", tag="tok", bufs=3, align_bytes=64)
             src = tiles[holder[gate], u][:].rearrange("p (j m t) -> p m j t", j=PACK, t=PACK)[:, m0:m1]
             dst = tiles["tok", gate, u][:].rearrange("p (t m j) -> p m j t", j=PACK, t=PACK)[:, m0:m1]
-            if gate == GATE_N:
+            if gate == GATE_N and on_vector:
+                nc.vector.tensor_scalar(out=dst, in0=src, scalar1=MEAN_SHARE, scalar2=None, op0=ALU.mult)
+            elif gate == GATE_N:
                 nc.scalar.activation(out=dst, in_=src, func=ACT.Copy, scale=MEAN_SHARE)
             elif on_vector:
                 nc.vector.tensor_copy(out=dst, in_=src)
@@ -237,7 +241,7 @@ def tile_fractalengine_pb_v_kernel(
             group_features(gate, u, 1)
 
         def quantise_features(gate, u, half=None):
-            quantise(("feat", gate, u), tiles["feat", gate, u], E5M2, "kept" if u == 1 else "feat", 3, half)
+            quantise(("feat", gate, u), tiles["feat", gate, u], E5M2, "feat", 3, half)
 
         def load_eng(g):
             tiles["eng_raw", g] = work.tile([P, UNIT], BF16, name="raw", tag="raw", bufs=3)
@@ -275,9 +279,10 @@ def tile_fractalengine_pb_v_kernel(
                         words[:, 2 * P * dt + k % 2 : 2 * P * (dt + 1) : 2], ident[:],
                     )
 
-        def group_w(gate, c):
-            tiles["w", gate, c] = work.tile([P, UNIT], BF16, name="side", tag="side", bufs=2, align_bytes=64)
-            for pair in range(2):
+        def group_w(gate, c, pairs=(0, 1)):
+            if 0 in pairs:
+                tiles["w", gate, c] = work.tile([P, UNIT], BF16, name="side", tag="side", bufs=2, align_bytes=64)
+            for pair in pairs:
                 nc.scalar.copy(
                     out=tiles["w", gate, c][:, pair * 2 * W : (pair + 1) * 2 * W].bitcast(F32).rearrange("q (d r v) -> q d r v", d=2, v=2),
                     in_=tiles["w_turned", gate, c, pair][:].rearrange("q (d v r) -> q d r v", d=2, v=2),
@@ -330,13 +335,18 @@ def tile_fractalengine_pb_v_kernel(
                 lhsT_scale=tiles["scales", "feat", gate, u][:, j * P : (j + 1) * P],
                 rhs=tiles["codes", "w", gate, c][:].bitcast(E4M3),
                 rhs_scale=tiles["scales", "w", gate, c][:],
-                start=(b is not None), stop=(gate == GATE_R and c == 1),
+                start=(b is not None), stop=(gate == GATE_R and u != 1),
             )
 
-        def empty_input_grad(g, j, on_vector=False):
+        first_half = keep.tile([P, UNIT], F32, name="first_half")
+
+        def park_input_grad(j):
+            nc.scalar.copy(out=first_half[:, j * W : (j + 1) * W], in_=tiles["dx", 0, j][:])
+
+        def empty_input_grad(g, j):
             dst = staging(("dx_out", g))[:, j * W : (j + 1) * W]
-            if on_vector:
-                nc.vector.tensor_copy(out=dst, in_=tiles["dx", g, j][:])
+            if g == 0:
+                nc.vector.tensor_tensor(out=dst, in0=tiles["dx", g, j][:], in1=first_half[:, j * W : (j + 1) * W], op=ALU.add)
             else:
                 nc.scalar.copy(out=dst, in_=tiles["dx", g, j][:])
 
@@ -349,7 +359,7 @@ def tile_fractalengine_pb_v_kernel(
         def input_passes(gate, u, js=range(PACK)):
             c, g = UNITS[u]
             for j in js:
-                input_grad(g, j, gate, c, 4 + j if (gate == GATE_N and c == 0) else None)
+                input_grad(g, j, gate, c, 4 + j if (gate == GATE_N and u != 2) else None)
 
         waiting = []
         filled = []
@@ -367,7 +377,7 @@ def tile_fractalengine_pb_v_kernel(
 
         def queue_dw(gate, u):
             c, g = UNITS[u]
-            if g == 1:
+            if u % 2 == 1:
                 waiting.extend([(gate, c, dt) for dt in range(PACK)])
 
         def w_pass(gate, c):
@@ -382,184 +392,214 @@ def tile_fractalengine_pb_v_kernel(
         load("n", 0, 0)
         load("h", 0, 0)
         load("z", 0, 0)
+        load_eng(0)
         load("n", 0, 1)
         load("h", 0, 1)
         load("z", 0, 1)
         load_w(GATE_N, 0)
         load_tension()
         load("r", 0)
-        load_eng(0)
-        load("hn", 0)
+        load("g", 1)
         load_w(GATE_Z, 0)
+        load("n", 1)
+        load("h", 1)
+        load("hn", 0)
         faction_sums(0)
         n_minus_h(0, 0)
         square_n(0, 0)
         pull_back(0, 0)
         pull_back(0, 1)
+        group_eng(0)
+        load_eng(1)
+        load("z", 1)
         through_z(0, 0)
         n_minus_h(0, 1)
         square_n(0, 1)
         through_z(0, 1)
         widen_tension()
         w_pass(GATE_N, 0)
-        for name in ("g", "n", "h", "z"):
-            load(name, 1)
         load_w(GATE_R, 0)
         load("r", 1)
         load("hn", 1)
         finish_dn(0, 0)
-        square_r(0)
         finish_dn(0, 1)
 
         for u in range(len(UNITS)):
             c, g = UNITS[u]
             last = u == len(UNITS) - 1
             if u > 0:
-                n_minus_h(u)
-                last_row_sums(GATE_R, u - 1, range(2))
-                quantise_features(GATE_Z, u - 1)
-                square_n(u)
-                turn(GATE_R, u - 1)
-                if g == 1:
-                    input_passes(GATE_Z, u - 1)
-                pull_back(u)
-                quantise_tokens(GATE_R, u - 1)
-                last_row_sums(GATE_R, u - 1, range(2, 4))
-                queue_dw(GATE_Z, u - 1)
-                queue_dw(GATE_R, u - 1)
-                next_dw()
-                if not last:
-                    for name in ("g", "n", "h", "z", "r", "hn"):
-                        load(name, u + 1)
-                group_features(GATE_R, u - 1, 0)
-                next_dw()
-                group_features(GATE_R, u - 1, 1)
-                next_dw()
                 through_z(u)
+                if not last:
+                    load("n", u + 1)
+                last_row_sums(GATE_R, u - 1, range(2))
+                round_tokens(GATE_R, u - 1, on_vector=(u > 1))
+                next_dw()
+                if u == 1:
+                    quantise_eng(1)
+                quantise_features(GATE_Z, u - 1)
+                queue_dw(GATE_Z, u - 1)
+                turn(GATE_R, u - 1)
                 square_r(u, 0)
                 next_dw()
-                square_r(u, 1)
+                input_passes(GATE_Z, u - 1)
+                if not last:
+                    square_r(u, 1)
                 next_dw()
-                quantise_features(GATE_R, u - 1)
-                if g == 1:
-                    input_passes(GATE_R, u - 1)
+                quantise_tokens(GATE_R, u - 1)
+                last_row_sums(GATE_R, u - 1, range(2, 3))
+                group_features(GATE_R, u - 1, 0)
+                next_dw()
+                last_row_sums(GATE_R, u - 1, range(3, 4))
+                group_features(GATE_R, u - 1, 1)
+                next_dw()
+                if not last:
+                    load("r", u + 1)
                 finish_dn(u)
                 if u == 1:
-                    group_eng(1)
-                    load_w(GATE_Z, 1)
+                    turn_w(GATE_R, 0)
                 if u == 2:
                     empty_last_row(0)
-                    next_dw()
-                if u == 3:
-                    for j in range(PACK):
-                        empty_input_grad(0, j)
-                    store_input_grad(0, slice(0, PACK))
+            if last:
+                break
             last_row_sums(GATE_N, u, range(2))
-            round_tokens(GATE_N, u, False, 0, P // 2)
+            round_tokens(GATE_N, u)
             next_dw()
-            last_row_sums(GATE_N, u, range(2, 4))
-            round_tokens(GATE_N, u, False, P // 2, P)
-            next_dw()
+            if u == 1:
+                group_w(GATE_R, 0)
+                load_w(GATE_Z, 1)
+                load_w(GATE_R, 1)
+            faction_sums(u + 1)
             times_z(u)
-            turn(GATE_N, u)
+            if u > 0:
+                quantise_features(GATE_R, u - 1)
             if u == 0:
                 quantise_w(GATE_N, 0)
-                group_eng(0)
-                load_eng(1)
-            if u == 1:
-                quantise_eng(1)
-            if u == 3:
-                input_passes(GATE_N, 1)
-                input_passes(GATE_Z, 1)
-            next_dw()
-            if not last:
-                times_hn(u)
-            quantise_tokens(GATE_N, u)
-            queue_dw(GATE_N, u)
-            next_dw()
-            group_features(GATE_N, u, 0)
-            next_dw()
-            group_features(GATE_N, u, 1)
-            next_dw()
-            finish_dz(u)
-            if last:
-                times_hn(u)
-                input_passes(GATE_R, 1)
-            if u == 0:
                 quantise_eng(0)
-                w_pass(GATE_Z, 0)
-                load_w(GATE_N, 1)
+            turn(GATE_N, u)
+            finish_dz(u)
+            quantise_tokens(GATE_N, u)
+            if u == 1:
+                quantise_w(GATE_R, 0)
             if u == 2:
-                w_pass(GATE_Z, 1)
+                quantise_w(GATE_N, 1)
+            if u > 0:
+                input_passes(GATE_R, u - 1)
+            last_row_sums(GATE_N, u, range(2, 4))
+            if u == 0:
+                square_r(0)
+            if u > 0:
+                round_tokens(GATE_Z, u)
+            if u == 1:
+                for j in range(PACK):
+                    park_input_grad(j)
+            group_both(GATE_N, u)
+            n_minus_h(u + 1)
+            if u != 1:
+                w_pass(GATE_Z, c)
             last_row_sums(GATE_Z, u, range(2))
+            if u == 0:
+                load_w(GATE_N, 1)
+                round_tokens(GATE_Z, u)
+            pull_back(u + 1)
+            if u + 2 < len(UNITS):
+                for name in ("g", "h", "z"):
+                    load(name, u + 2)
+            if u == 1:
+                queue_dw(GATE_N, 1)
+            if u == 2:
+                queue_dw(GATE_R, 1)
             next_dw()
-            if last:
-                round_tokens(GATE_Z, u, True)
-                quantise_features(GATE_N, u)
-                next_dw()
-                turn(GATE_Z, u)
-                input_passes(GATE_N, u)
-                quantise_tokens(GATE_Z, u)
-                last_row_sums(GATE_Z, u, range(2, 4))
-                finish_dr(u)
+            turn(GATE_Z, u)
+            times_hn(u)
+            if u + 2 < len(UNITS):
+                load("hn", u + 2)
+            square_n(u + 1, 0)
+            next_dw()
+            quantise_features(GATE_N, u)
+            if u != 1:
+                quantise_w(GATE_Z, c)
+            last_row_sums(GATE_Z, u, range(2, 3))
+            square_n(u + 1, 1)
+            next_dw()
+            input_passes(GATE_N, u)
+            quantise_tokens(GATE_Z, u)
+            group_features(GATE_Z, u, 0)
+            next_dw()
+            group_features(GATE_Z, u, 1)
+            if u == 0:
+                group_eng(1)
             else:
-                quantise_features(GATE_N, u)
-                round_shared(GATE_Z, u, P // 2)
-                next_dw(refill=False)
-                last_row_sums(GATE_Z, u, range(2, 4))
-                if u == 0:
-                    quantise_w(GATE_Z, 0)
-                    w_pass(GATE_R, 0)
-                if u == 1:
-                    w_pass(GATE_N, 1)
-                    load_w(GATE_R, 1)
-                if u == 2:
-                    quantise_w(GATE_Z, 1)
-                    w_pass(GATE_R, 1)
-                finish_dr(u)
-                turn(GATE_Z, u)
-                if g == 0:
-                    input_passes(GATE_N, u)
-                faction_sums(u + 1)
-                quantise_tokens(GATE_Z, u)
-                quantise_w(GATE_N if u == 1 else GATE_R, 1 if u > 0 else 0)
-                group_both(GATE_Z, u)
-                round_tokens(GATE_R, u)
+                w_pass(GATE_N if u == 1 else GATE_R, 1)
+            last_row_sums(GATE_Z, u, range(3, 4))
+            finish_dr(u)
 
         u = len(UNITS) - 1
-        queue_dw(GATE_Z, u)
-        next_dw()
-        group_features(GATE_Z, u, 0)
-        next_dw()
-        group_features(GATE_Z, u, 1)
-        next_dw()
-        round_shared(GATE_R, u, 96)
+        quantise_w(GATE_R, 1)
+        quantise_features(GATE_R, u - 1)
+        input_passes(GATE_R, u - 1)
+        square_r(u, 1)
+        round_tokens(GATE_N, u)
+        last_row_sums(GATE_N, u, range(1))
+        times_z(u)
+        turn(GATE_N, u)
+        quantise_tokens(GATE_N, u)
+        weight_grad(GATE_N, 1, 0, 3)
+        for j in range(PACK):
+            empty_input_grad(1, j)
+        store_input_grad(1, slice(0, PACK))
+        for dt in range(1, PACK):
+            weight_grad(GATE_N, 1, dt, 3 + dt)
+        finish_dz(u)
+        last_row_sums(GATE_N, u, range(1, 3))
+        group_both(GATE_N, u)
+        round_tokens(GATE_Z, u, on_vector=True)
+        turn(GATE_Z, u)
+        last_row_sums(GATE_N, u, range(3, 4))
+        times_hn(u)
+        for dt in range(PACK):
+            empty_weight_grad(GATE_N, 1, dt)
+        store_weight_grad(GATE_N, 1, slice(0, PACK))
+        last_row_sums(GATE_Z, u, range(2))
+        quantise_tokens(GATE_Z, u)
+        weight_grad(GATE_Z, 1, 0, 3)
+        weight_grad(GATE_Z, 1, 1, 7)
+        quantise_features(GATE_N, u)
+        input_passes(GATE_N, u, range(3))
+        group_both(GATE_Z, u)
+        finish_dr(u)
+        empty_weight_grad(GATE_Z, 1, 0)
+        weight_grad(GATE_Z, 1, 2, 3)
+        empty_weight_grad(GATE_Z, 1, 1)
+        store_weight_grad(GATE_Z, 1, slice(0, 2))
+        weight_grad(GATE_Z, 1, 3, 7)
         quantise_features(GATE_Z, u)
-        next_dw()
+        input_passes(GATE_Z, u, range(3))
+        round_tokens(GATE_R, u, on_vector=True)
+        empty_weight_grad(GATE_Z, 1, 2)
+        empty_weight_grad(GATE_Z, 1, 3)
+        store_weight_grad(GATE_Z, 1, slice(2, 4))
         turn(GATE_R, u)
         quantise_tokens(GATE_R, u)
-        next_dw()
-        input_passes(GATE_Z, u)
+        input_passes(GATE_N, u, range(3, 4))
+        input_passes(GATE_Z, u, range(3, 4))
         weight_grad(GATE_R, 1, 0, 3)
         group_features(GATE_R, u, 0)
         group_features(GATE_R, u, 1, on_vector=True)
         weight_grad(GATE_R, 1, 1, 1)
         empty_weight_grad(GATE_R, 1, 0)
-        quantise_features(GATE_R, u)
         weight_grad(GATE_R, 1, 2, 2)
-        input_passes(GATE_R, u)
+        quantise_features(GATE_R, u)
         weight_grad(GATE_R, 1, 3, 3)
-        last_row_sums(GATE_R, u)
         empty_weight_grad(GATE_R, 1, 1)
         store_weight_grad(GATE_R, 1, slice(0, 2))
-        empty_weight_grad(GATE_R, 1, 2, on_vector=True)
-        empty_input_grad(1, 0)
-        empty_input_grad(1, 1, on_vector=True)
-        store_input_grad(1, slice(0, 2))
-        empty_input_grad(1, 2)
-        empty_input_grad(1, 3, on_vector=True)
-        store_input_grad(1, slice(2, 4))
+        input_passes(GATE_R, u)
+        last_row_sums(GATE_Z, u, range(2, 4))
+        last_row_sums(GATE_R, u)
+        empty_weight_grad(GATE_R, 1, 2)
         empty_weight_grad(GATE_R, 1, 3)
         store_weight_grad(GATE_R, 1, slice(2, 4))
+        for j in range(PACK):
+            empty_input_grad(0, j)
+            store_input_grad(0, slice(j, j + 1))
         empty_last_row(1)
         store_last_row()

@@ -26,6 +26,9 @@ MEAN_SHARE = SYNC / FACTION
 OWN_OVER_MEAN = (1.0 - SYNC) / MEAN_SHARE
 GATE_R, GATE_Z, GATE_N = 0, 1, 2
 LAST_WIDE = 40
+FOLDED = {(1, 2), (1, 3), (0, 3)}
+RVEC = (2,)
+BLOCKS = 3 * DHID // P
 R_SPLIT = 64
 TAIL_SPLIT = 88
 UNITS = [(0, 0), (0, 1), (1, 1), (1, 0)]
@@ -46,6 +49,15 @@ def tile_fractalengine_pb_v_kernel(
         make_block_diagonal(nc, same_f32[:], FACTION // PACK)
         last_cols = keep.tile([P, P], F32, name="last_cols")
         nc.gpsimd.memset(last_cols[:], 0.0)
+        ten = keep.tile([P, 2 * PACK, LAST_WIDE], F32, name="ten")
+        ten_n = keep.tile([P, 2 * PACK, LAST_WIDE], F32, name="ten_n")
+        ten_first = keep.tile([P, BLOCKS + LAST_WIDE], F32, name="ten_first")
+        nc.gpsimd.memset(ten[:], 0.0)
+        nc.gpsimd.memset(ten_n[:], 0.0)
+        nc.gpsimd.memset(ten_first[:], 0.0)
+        one_column = keep.tile([P, LAST_WIDE], F32, name="one_column")
+        nc.gpsimd.memset(one_column[:], 0.0)
+        nc.gpsimd.memset(one_column[:, 0:1], 1.0)
 
         ctx.enter_context(tc.manual_schedule())
 
@@ -147,41 +159,65 @@ def tile_fractalengine_pb_v_kernel(
         holder = {GATE_R: "r", GATE_Z: "dz", GATE_N: "n"}
 
         ten_raw = keep.tile([P, 2, PACK], BF16, name="ten_raw")
-        ten = keep.tile([P, 2 * PACK, LAST_WIDE], F32, name="ten")
-        ten_n = keep.tile([P, 2 * PACK, LAST_WIDE], F32, name="ten_n")
+        last_acc = bank(0, "last_acc")
 
         def load_tension():
             nc.sync.dma_start(out=ten_raw[:], in_=tension.rearrange("(g p j) -> p g j", p=P, j=PACK))
 
         def widen_tension():
-            wide = ten_raw[:].rearrange("p g j -> p (g j)").unsqueeze(2).to_broadcast([P, 2 * PACK, LAST_WIDE])
-            nc.scalar.activation(out=ten[:], in_=wide, func=ACT.Copy)
-            nc.scalar.activation(out=ten_n[:], in_=wide, func=ACT.Copy, scale=MEAN_SHARE)
+            flat = ten_raw[:].rearrange("p g j -> p (g j)")
+            nc.scalar.activation(out=ten[:, :, 0], in_=flat, func=ACT.Copy)
+            nc.scalar.activation(out=ten_n[:, :, 0], in_=flat, func=ACT.Copy, scale=MEAN_SHARE)
+            col = GATE_N * 2 * PACK
+            nc.scalar.activation(out=ten_first[:, col : col + 1], in_=flat[:, 0:1], func=ACT.Copy, scale=MEAN_SHARE)
 
         def last_row_sums(gate, u, fbs=range(PACK)):
             c, g = UNITS[u]
             weights = ten_n if gate == GATE_N else ten
+            if (gate, u) in FOLDED:
+                return
             for fb in fbs:
-                if gate == GATE_N and fb == 0 and u % 2 == 0:
-                    tiles["last", c] = bank(0, "last_acc")
-                col = (gate * PACK + fb) * LAST_WIDE
                 for j in range(PACK):
+                    first = u == 0 and gate == GATE_N and fb == 0 and j == 0
+                    col = (gate * 2 + c) * PACK + fb
                     nc.tensor.matmul(
-                        out=tiles["last", c][:, col : col + LAST_WIDE],
+                        out=last_acc[:, :BLOCKS + LAST_WIDE] if first else last_acc[:, col : col + LAST_WIDE],
                         lhsT=tiles[holder[gate], u][:, j * W + fb * P : j * W + (fb + 1) * P],
-                        rhs=weights[:, g * PACK + j, :],
-                        start=(u % 2 == 0 and gate == GATE_N and fb == 0 and j == 0),
-                        stop=(u % 2 == 1 and gate == GATE_R and fb == PACK - 1 and j == PACK - 1),
+                        rhs=ten_first[:] if first else weights[:, g * PACK + j, :],
+                        start=first,
+                        stop=(u == len(UNITS) - 1 and gate == GATE_R and fb == PACK - 1 and j == PACK - 1),
                     )
 
-        def empty_last_row(c):
-            nc.scalar.copy(
-                out=last_cols[:, : 6 * PACK].rearrange("p (gate c fb) -> p gate c fb", c=2, fb=PACK)[:, :, c, :],
-                in_=tiles["last", c][:, : 3 * PACK * LAST_WIDE].rearrange("p (gate fb n) -> p gate fb n", fb=PACK, n=LAST_WIDE)[:, :, :, 0],
-            )
+        def fold_slots(gate, u, js=range(PACK)):
+            c, g = UNITS[u]
+            weights = ten_n if gate == GATE_N else ten
+            if (gate, u) not in FOLDED:
+                return
+            folded = tiles["z", u][:, gate * W : (gate + 1) * W]
+            for j in js:
+                slot = tiles[holder[gate], u][:, j * W : (j + 1) * W]
+                weight = weights[:, g * PACK + j, 0:1]
+                if j == 0:
+                    nc.vector.tensor_scalar(out=folded, in0=slot, scalar1=weight, scalar2=None, op0=ALU.mult)
+                else:
+                    nc.vector.scalar_tensor_tensor(out=folded, in0=slot, scalar=weight, in1=folded, op0=ALU.mult, op1=ALU.add)
+
+        def folded_sums(gate, u):
+            c, g = UNITS[u]
+            if (gate, u) not in FOLDED:
+                return
+            for fb in range(PACK):
+                col = (gate * 2 + c) * PACK + fb
+                nc.tensor.matmul(
+                    out=last_acc[:, col : col + LAST_WIDE],
+                    lhsT=tiles["z", u][:, gate * W + fb * P : gate * W + (fb + 1) * P],
+                    rhs=one_column[:], start=False,
+                    stop=(u == len(UNITS) - 1 and gate == GATE_R and fb == PACK - 1),
+                )
 
         def store_last_row():
-            blocks = 3 * DHID // P
+            blocks = BLOCKS
+            nc.scalar.copy(out=last_cols[:, :BLOCKS], in_=last_acc[:, :BLOCKS])
             turned = bank(0, "last_turned")
             nc.tensor.transpose(turned[:, :P], last_cols[:], ident[:])
             last_rows = keep.tile([32, P], F32, name="last_rows")
@@ -411,7 +447,6 @@ def tile_fractalengine_pb_v_kernel(
         pull_back(0, 1)
         group_eng(0)
         load_eng(1)
-        load("z", 1)
         through_z(0, 0)
         n_minus_h(0, 1)
         square_n(0, 1)
@@ -419,6 +454,7 @@ def tile_fractalengine_pb_v_kernel(
         widen_tension()
         w_pass(GATE_N, 0)
         load_w(GATE_R, 0)
+        load("z", 1)
         load("r", 1)
         load("hn", 1)
         finish_dn(0, 0)
@@ -431,79 +467,93 @@ def tile_fractalengine_pb_v_kernel(
                 through_z(u)
                 if not last:
                     load("n", u + 1)
+                    load("z", u + 1)
                 last_row_sums(GATE_R, u - 1, range(2))
-                round_tokens(GATE_R, u - 1, on_vector=(u > 1))
+                round_tokens(GATE_R, u - 1, on_vector=(u in RVEC))
                 next_dw()
-                if u == 1:
-                    quantise_eng(1)
                 quantise_features(GATE_Z, u - 1)
-                queue_dw(GATE_Z, u - 1)
                 turn(GATE_R, u - 1)
-                square_r(u, 0)
+                if u < 3:
+                    square_r(u)
+                finish_dn(u)
+                queue_dw(GATE_Z, u - 1)
                 next_dw()
                 input_passes(GATE_Z, u - 1)
-                if not last:
-                    square_r(u, 1)
-                next_dw()
-                quantise_tokens(GATE_R, u - 1)
+                if u == 2:
+                    round_tokens(GATE_N, u)
+                    next_dw()
                 last_row_sums(GATE_R, u - 1, range(2, 3))
                 group_features(GATE_R, u - 1, 0)
                 next_dw()
                 last_row_sums(GATE_R, u - 1, range(3, 4))
                 group_features(GATE_R, u - 1, 1)
-                next_dw()
                 if not last:
                     load("r", u + 1)
-                finish_dn(u)
                 if u == 1:
                     turn_w(GATE_R, 0)
-                if u == 2:
-                    empty_last_row(0)
             if last:
                 break
+            if u == 0:
+                square_r(0)
+            if u == 2:
+                next_dw()
+                turn(GATE_N, u)
+                next_dw()
+                faction_sums(u + 1)
             last_row_sums(GATE_N, u, range(2))
-            round_tokens(GATE_N, u)
-            next_dw()
+            if u < 2:
+                round_tokens(GATE_N, u)
             if u == 1:
                 group_w(GATE_R, 0)
                 load_w(GATE_Z, 1)
                 load_w(GATE_R, 1)
-            faction_sums(u + 1)
+            if u < 2:
+                faction_sums(u + 1)
             times_z(u)
             if u > 0:
-                quantise_features(GATE_R, u - 1)
-            if u == 0:
+                quantise_tokens(GATE_R, u - 1)
+            else:
                 quantise_w(GATE_N, 0)
                 quantise_eng(0)
-            turn(GATE_N, u)
+            if u < 2:
+                turn(GATE_N, u)
             finish_dz(u)
-            quantise_tokens(GATE_N, u)
+            last_row_sums(GATE_N, u, range(2, 3))
             if u == 1:
+                quantise_eng(1)
                 quantise_w(GATE_R, 0)
             if u == 2:
                 quantise_w(GATE_N, 1)
             if u > 0:
+                quantise_features(GATE_R, u - 1)
                 input_passes(GATE_R, u - 1)
-            last_row_sums(GATE_N, u, range(2, 4))
-            if u == 0:
-                square_r(0)
-            if u > 0:
-                round_tokens(GATE_Z, u)
+            quantise_tokens(GATE_N, u)
+            if u < 2:
+                last_row_sums(GATE_N, u, range(3, 4))
+            round_tokens(GATE_Z, u)
+            group_features(GATE_N, u, 0)
             if u == 1:
                 for j in range(PACK):
                     park_input_grad(j)
-            group_both(GATE_N, u)
+            group_features(GATE_N, u, 1)
             n_minus_h(u + 1)
-            if u != 1:
-                w_pass(GATE_Z, c)
+            if u == 2:
+                turn_w(GATE_Z, c)
+                last_row_sums(GATE_N, u, range(3, 4))
             last_row_sums(GATE_Z, u, range(2))
             if u == 0:
-                load_w(GATE_N, 1)
-                round_tokens(GATE_Z, u)
+                turn_w(GATE_Z, c)
+            fold_slots(GATE_Z, u, [0])
             pull_back(u + 1)
+            fold_slots(GATE_Z, u, [1])
             if u + 2 < len(UNITS):
-                for name in ("g", "h", "z"):
-                    load(name, u + 2)
+                load("g", u + 2)
+                load("h", u + 2)
+            square_n(u + 1, 0)
+            if u != 1:
+                group_w(GATE_Z, c)
+            if u == 0:
+                load_w(GATE_N, 1)
             if u == 1:
                 queue_dw(GATE_N, 1)
             if u == 2:
@@ -511,59 +561,70 @@ def tile_fractalengine_pb_v_kernel(
             next_dw()
             turn(GATE_Z, u)
             times_hn(u)
+            fold_slots(GATE_Z, u, [2])
             if u + 2 < len(UNITS):
                 load("hn", u + 2)
-            square_n(u + 1, 0)
-            next_dw()
-            quantise_features(GATE_N, u)
-            if u != 1:
-                quantise_w(GATE_Z, c)
             last_row_sums(GATE_Z, u, range(2, 3))
             square_n(u + 1, 1)
             next_dw()
-            input_passes(GATE_N, u)
             quantise_tokens(GATE_Z, u)
+            quantise_features(GATE_N, u)
+            fold_slots(GATE_Z, u, [3])
+            if u != 1:
+                quantise_w(GATE_Z, c)
+            if u == 2:
+                square_r(3, 0)
+            input_passes(GATE_N, u)
+            if u == 0:
+                group_eng(1)
             group_features(GATE_Z, u, 0)
             next_dw()
             group_features(GATE_Z, u, 1)
-            if u == 0:
-                group_eng(1)
-            else:
-                w_pass(GATE_N if u == 1 else GATE_R, 1)
+            if u > 0:
+                turn_w(GATE_N if u == 1 else GATE_R, 1)
+                next_dw()
+                group_w(GATE_N if u == 1 else GATE_R, 1)
             last_row_sums(GATE_Z, u, range(3, 4))
+            folded_sums(GATE_Z, u)
             finish_dr(u)
 
         u = len(UNITS) - 1
         quantise_w(GATE_R, 1)
-        quantise_features(GATE_R, u - 1)
-        input_passes(GATE_R, u - 1)
         square_r(u, 1)
         round_tokens(GATE_N, u)
         last_row_sums(GATE_N, u, range(1))
         times_z(u)
+        quantise_tokens(GATE_R, u - 1)
+        quantise_features(GATE_R, u - 1)
+        input_passes(GATE_R, u - 1)
         turn(GATE_N, u)
+        finish_dz(u)
         quantise_tokens(GATE_N, u)
+        last_row_sums(GATE_N, u, range(1, 2))
         weight_grad(GATE_N, 1, 0, 3)
         for j in range(PACK):
             empty_input_grad(1, j)
         store_input_grad(1, slice(0, PACK))
         for dt in range(1, PACK):
             weight_grad(GATE_N, 1, dt, 3 + dt)
-        finish_dz(u)
-        last_row_sums(GATE_N, u, range(1, 3))
+        last_row_sums(GATE_N, u, range(2, 3))
         group_both(GATE_N, u)
         round_tokens(GATE_Z, u, on_vector=True)
         turn(GATE_Z, u)
         last_row_sums(GATE_N, u, range(3, 4))
+        fold_slots(GATE_Z, u, [0])
         times_hn(u)
+        fold_slots(GATE_Z, u, [1])
         for dt in range(PACK):
             empty_weight_grad(GATE_N, 1, dt)
         store_weight_grad(GATE_N, 1, slice(0, PACK))
         last_row_sums(GATE_Z, u, range(2))
         quantise_tokens(GATE_Z, u)
+        fold_slots(GATE_Z, u, [2])
         weight_grad(GATE_Z, 1, 0, 3)
         weight_grad(GATE_Z, 1, 1, 7)
         quantise_features(GATE_N, u)
+        fold_slots(GATE_Z, u, [3])
         input_passes(GATE_N, u, range(3))
         group_both(GATE_Z, u)
         finish_dr(u)
@@ -572,34 +633,49 @@ def tile_fractalengine_pb_v_kernel(
         empty_weight_grad(GATE_Z, 1, 1)
         store_weight_grad(GATE_Z, 1, slice(0, 2))
         weight_grad(GATE_Z, 1, 3, 7)
-        quantise_features(GATE_Z, u)
-        input_passes(GATE_Z, u, range(3))
-        round_tokens(GATE_R, u, on_vector=True)
+        round_shared(GATE_R, u, TAIL_SPLIT)
+        folded_sums(GATE_Z, u)
+        turn(GATE_R, u)
         empty_weight_grad(GATE_Z, 1, 2)
         empty_weight_grad(GATE_Z, 1, 3)
         store_weight_grad(GATE_Z, 1, slice(2, 4))
-        turn(GATE_R, u)
+        quantise_features(GATE_Z, u)
         quantise_tokens(GATE_R, u)
-        input_passes(GATE_N, u, range(3, 4))
-        input_passes(GATE_Z, u, range(3, 4))
+        input_passes(GATE_Z, u, range(2))
+        fold_slots(GATE_R, u, [0])
         weight_grad(GATE_R, 1, 0, 3)
         group_features(GATE_R, u, 0)
-        group_features(GATE_R, u, 1, on_vector=True)
+        quantise_features(GATE_R, u, 0)
+        input_passes(GATE_R, u, range(2))
+        fold_slots(GATE_R, u, [1])
+        group_features(GATE_R, u, 1)
         weight_grad(GATE_R, 1, 1, 1)
+        input_passes(GATE_Z, u, range(2, 3))
+        input_passes(GATE_N, u, range(3, 4))
+        input_passes(GATE_Z, u, range(3, 4))
+        empty_input_grad(0, 0)
+        store_input_grad(0, slice(0, 1))
+        fold_slots(GATE_R, u, [2])
+        quantise_features(GATE_R, u, 1)
         empty_weight_grad(GATE_R, 1, 0)
+        store_weight_grad(GATE_R, 1, slice(0, 1))
         weight_grad(GATE_R, 1, 2, 2)
-        quantise_features(GATE_R, u)
+        input_passes(GATE_R, u, range(2, 4))
         weight_grad(GATE_R, 1, 3, 3)
+        fold_slots(GATE_R, u, [3])
         empty_weight_grad(GATE_R, 1, 1)
-        store_weight_grad(GATE_R, 1, slice(0, 2))
-        input_passes(GATE_R, u)
+        store_weight_grad(GATE_R, 1, slice(1, 2))
         last_row_sums(GATE_Z, u, range(2, 4))
         last_row_sums(GATE_R, u)
+        folded_sums(GATE_R, u)
+        empty_input_grad(0, 1)
+        store_input_grad(0, slice(1, 2))
         empty_weight_grad(GATE_R, 1, 2)
+        store_weight_grad(GATE_R, 1, slice(2, 3))
+        empty_input_grad(0, 2)
+        store_input_grad(0, slice(2, 3))
         empty_weight_grad(GATE_R, 1, 3)
-        store_weight_grad(GATE_R, 1, slice(2, 4))
-        for j in range(PACK):
-            empty_input_grad(0, j)
-            store_input_grad(0, slice(j, j + 1))
-        empty_last_row(1)
+        store_weight_grad(GATE_R, 1, slice(3, 4))
         store_last_row()
+        empty_input_grad(0, 3)
+        store_input_grad(0, slice(3, 4))

from contextlib import ExitStack

import concourse.mybir as mybir
from concourse.masks import make_block_diagonal, make_identity

N, DHID, DOUT = 1024, 1024, 512
FACTION = 32
SYNC = 0.15
FLOPS = 2 * 2 * N * 3 * DHID * DOUT
BYTES = (N * DOUT + N + 2 * N * DHID + DOUT * 3 * DHID) * 2 + 4 * N * DHID * 4 + (N * DOUT + (DOUT + 1) * 3 * DHID) * 4

F32 = mybir.dt.float32
BF16 = mybir.dt.bfloat16
U32 = mybir.dt.uint32
U8 = mybir.dt.uint8
E4M3 = mybir.dt.float8_e4m3fn_x4
E5M2 = mybir.dt.float8_e5m2_x4
ALU = mybir.AluOpType
ACT = mybir.ActivationFunctionType

P = 128
PACK = 4
W = P * PACK
UNIT = PACK * W
MEAN_SHARE = SYNC / FACTION
OWN_OVER_MEAN = (1.0 - SYNC) / MEAN_SHARE
GATE_R, GATE_Z, GATE_N = 0, 1, 2
LAST_WIDE = 40
FOLDED = {(1, 2), (1, 3), (0, 3)}
RVEC = (2,)
BLOCKS = 3 * DHID // P
R_SPLIT = 64
TAIL_SPLIT = 88
UNITS = [(0, 0), (0, 1), (1, 1), (1, 0)]


def tile_fractalengine_pb_v_kernel(
    tc, eng_out, tension, hiddens, w_ih, b_ih, w_hh, b_hh, rz, ncand, hn, grad_out, out_0, out_1
):
    nc = tc.nc
    with ExitStack() as ctx:
        keep = ctx.enter_context(tc.tile_pool(name="keep", bufs=1))
        work = ctx.enter_context(tc.tile_pool(name="work", bufs=2))
        psum = ctx.enter_context(tc.psum_pool(name="psum", bufs=1))

        ident = keep.tile([P, P], F32, name="ident")
        make_identity(nc, ident[:])
        same_f32 = keep.tile([P, P], F32, name="same_f32")
        make_block_diagonal(nc, same_f32[:], FACTION // PACK)
        last_cols = keep.tile([P, P], F32, name="last_cols")
        nc.gpsimd.memset(last_cols[:], 0.0)
        ten = keep.tile([P, 2 * PACK, LAST_WIDE], F32, name="ten")
        ten_n = keep.tile([P, 2 * PACK, LAST_WIDE], F32, name="ten_n")
        ten_first = keep.tile([P, BLOCKS + LAST_WIDE], F32, name="ten_first")
        nc.gpsimd.memset(ten[:], 0.0)
        nc.gpsimd.memset(ten_n[:], 0.0)
        nc.gpsimd.memset(ten_first[:], 0.0)
        one_column = keep.tile([P, LAST_WIDE], F32, name="one_column")
        nc.gpsimd.memset(one_column[:], 0.0)
        nc.gpsimd.memset(one_column[:, 0:1], 1.0)

        ctx.enter_context(tc.manual_schedule())

        same_faction = keep.tile([P, P], BF16, name="same_faction")
        nc.scalar.activation(out=same_faction[:], in_=same_f32[:], func=ACT.Square)

        sources = {
            "n": (ncand, 0, F32),
            "h": (hiddens, 0, BF16),
            "g": (grad_out, 0, BF16),
            "z": (rz, DHID, F32),
            "r": (rz, 0, F32),
            "hn": (hn, 0, F32),
        }
        tiles = {}

        def bank(b, name):
            return psum.tile([P, W], F32, name=name, tag="bank%d" % b)

        def by_slot(ap):
            return ap.rearrange("p (j f) -> p j f", f=W)

        def load(name, u, half=None):
            c, g = UNITS[u]
            src, col0, dtype = sources[name]
            if (name, u) not in tiles:
                tiles[name, u] = work.tile([P, UNIT], dtype, name="in_" + name, tag="in_" + name)
            rows = src[g * W : (g + 1) * W, col0 + c * W : col0 + (c + 1) * W].rearrange("(p j) f -> p j f", j=PACK)
            j0, j1 = (0, PACK) if half is None else (2 * half, 2 * half + 2)
            nc.sync.dma_start(out=by_slot(tiles[name, u][:, j0 * W : j1 * W]), in_=rows[:, j0:j1, :])

        def part(name, u, half):
            j0, j1 = (0, PACK) if half is None else (2 * half, 2 * half + 2)
            return tiles[name, u][:, j0 * W : j1 * W]

        def fresh(name, u, bufs):
            if (name, u) not in tiles:
                tiles[name, u] = work.tile([P, UNIT], F32, name=name, tag=name, bufs=bufs)

        def faction_sums(u):
            tiles["sums", u] = bank(3, "sums")
            for j in range(PACK):
                nc.tensor.matmul(
                    out=tiles["sums", u][:], lhsT=same_faction[:], rhs=tiles["g", u][:, j * W : (j + 1) * W],
                    start=(j == 0), stop=(j == PACK - 1),
                )

        def n_minus_h(u, half=None):
            fresh("dz", u, 2)
            nc.vector.tensor_tensor(out=part("dz", u, half), in0=part("n", u, half), in1=part("h", u, half), op=ALU.subtract)

        def pull_back(u, half=None):
            fresh("a", u, 1)
            slots = PACK if half is None else 2
            nc.vector.scalar_tensor_tensor(
                out=by_slot(part("a", u, half)), in0=by_slot(part("g", u, half)), scalar=OWN_OVER_MEAN,
                in1=tiles["sums", u][:].unsqueeze(1).to_broadcast([P, slots, W]), op0=ALU.mult, op1=ALU.add,
            )

        def through_z(u, half=None):
            nc.vector.scalar_tensor_tensor(
                out=part("a", u, half), in0=part("z", u, half), scalar=1.0, in1=part("a", u, half),
                op0=ALU.subtract, op1=ALU.mult,
            )

        def square_n(u, half=None):
            nc.scalar.activation(out=part("n", u, half), in_=part("n", u, half), func=ACT.Square)

        def finish_dn(u, half=None):
            nc.vector.scalar_tensor_tensor(
                out=part("n", u, half), in0=part("n", u, half), scalar=1.0, in1=part("a", u, half),
                op0=ALU.subtract, op1=ALU.mult,
            )

        def times_z(u, half=None):
            nc.vector.tensor_tensor(out=part("dz", u, half), in0=part("dz", u, half), in1=part("z", u, half), op=ALU.mult)

        def finish_dz(u):
            nc.vector.scalar_tensor_tensor(
                out=part("dz", u, None), in0=part("dz", u, None), scalar=MEAN_SHARE, in1=part("a", u, None),
                op0=ALU.mult, op1=ALU.mult,
            )

        def square_r(u, half=None):
            nc.scalar.activation(out=part("r", u, half), in_=part("r", u, half), func=ACT.Square, bias=-0.5)

        def times_hn(u):
            nc.vector.scalar_tensor_tensor(
                out=part("r", u, None), in0=part("r", u, None), scalar=0.25, in1=part("hn", u, None),
                op0=ALU.subtract, op1=ALU.mult,
            )

        def finish_dr(u):
            nc.vector.scalar_tensor_tensor(
                out=part("r", u, None), in0=part("r", u, None), scalar=-MEAN_SHARE, in1=part("n", u, None),
                op0=ALU.mult, op1=ALU.mult,
            )

        holder = {GATE_R: "r", GATE_Z: "dz", GATE_N: "n"}

        ten_raw = keep.tile([P, 2, PACK], BF16, name="ten_raw")
        last_acc = bank(0, "last_acc")

        def load_tension():
            nc.sync.dma_start(out=ten_raw[:], in_=tension.rearrange("(g p j) -> p g j", p=P, j=PACK))

        def widen_tension():
            flat = ten_raw[:].rearrange("p g j -> p (g j)")
            nc.scalar.activation(out=ten[:, :, 0], in_=flat, func=ACT.Copy)
            nc.scalar.activation(out=ten_n[:, :, 0], in_=flat, func=ACT.Copy, scale=MEAN_SHARE)
            col = GATE_N * 2 * PACK
            nc.scalar.activation(out=ten_first[:, col : col + 1], in_=flat[:, 0:1], func=ACT.Copy, scale=MEAN_SHARE)

        def last_row_sums(gate, u, fbs=range(PACK)):
            c, g = UNITS[u]
            weights = ten_n if gate == GATE_N else ten
            if (gate, u) in FOLDED:
                return
            for fb in fbs:
                for j in range(PACK):
                    first = u == 0 and gate == GATE_N and fb == 0 and j == 0
                    col = (gate * 2 + c) * PACK + fb
                    nc.tensor.matmul(
                        out=last_acc[:, :BLOCKS + LAST_WIDE] if first else last_acc[:, col : col + LAST_WIDE],
                        lhsT=tiles[holder[gate], u][:, j * W + fb * P : j * W + (fb + 1) * P],
                        rhs=ten_first[:] if first else weights[:, g * PACK + j, :],
                        start=first,
                        stop=(u == len(UNITS) - 1 and gate == GATE_R and fb == PACK - 1 and j == PACK - 1),
                    )

        def fold_slots(gate, u, js=range(PACK)):
            c, g = UNITS[u]
            weights = ten_n if gate == GATE_N else ten
            if (gate, u) not in FOLDED:
                return
            folded = tiles["z", u][:, gate * W : (gate + 1) * W]
            for j in js:
                slot = tiles[holder[gate], u][:, j * W : (j + 1) * W]
                weight = weights[:, g * PACK + j, 0:1]
                if j == 0:
                    nc.vector.tensor_scalar(out=folded, in0=slot, scalar1=weight, scalar2=None, op0=ALU.mult)
                else:
                    nc.vector.scalar_tensor_tensor(out=folded, in0=slot, scalar=weight, in1=folded, op0=ALU.mult, op1=ALU.add)

        def folded_sums(gate, u):
            c, g = UNITS[u]
            if (gate, u) not in FOLDED:
                return
            for fb in range(PACK):
                col = (gate * 2 + c) * PACK + fb
                nc.tensor.matmul(
                    out=last_acc[:, col : col + LAST_WIDE],
                    lhsT=tiles["z", u][:, gate * W + fb * P : gate * W + (fb + 1) * P],
                    rhs=one_column[:], start=False,
                    stop=(u == len(UNITS) - 1 and gate == GATE_R and fb == PACK - 1),
                )

        def store_last_row():
            blocks = BLOCKS
            nc.scalar.copy(out=last_cols[:, :BLOCKS], in_=last_acc[:, :BLOCKS])
            turned = bank(0, "last_turned")
            nc.tensor.transpose(turned[:, :P], last_cols[:], ident[:])
            last_rows = keep.tile([32, P], F32, name="last_rows")
            nc.scalar.copy(out=last_rows[:], in_=turned[:32, :P])
            nc.sync.dma_start(
                out=out_1[DOUT : DOUT + 1, :].rearrange("o (b f) -> (o b) f", f=P), in_=last_rows[:blocks, :]
            )

        def round_tokens(gate, u, on_vector=False, m0=0, m1=P):
            if ("tok", gate, u) not in tiles:
                tiles["tok", gate, u] = work.tile([P, UNIT], BF16, name="tok", tag="tok", bufs=3, align_bytes=64)
            src = tiles[holder[gate], u][:].rearrange("p (j m t) -> p m j t", j=PACK, t=PACK)[:, m0:m1]
            dst = tiles["tok", gate, u][:].rearrange("p (t m j) -> p m j t", j=PACK, t=PACK)[:, m0:m1]
            if gate == GATE_N and on_vector:
                nc.vector.tensor_scalar(out=dst, in0=src, scalar1=MEAN_SHARE, scalar2=None, op0=ALU.mult)
            elif gate == GATE_N:
                nc.scalar.activation(out=dst, in_=src, func=ACT.Copy, scale=MEAN_SHARE)
            elif on_vector:
                nc.vector.tensor_copy(out=dst, in_=src)
            else:
                nc.scalar.copy(out=dst, in_=src)

        def quantise(key, src, fmt, tag, bufs, half=None):
            if ("codes",) + key not in tiles:
                tiles[("codes",) + key] = work.tile([P, W], U32, name="codes_" + tag, tag="codes_" + tag, bufs=bufs, align_bytes=64)
                tiles[("scales",) + key] = work.tile([P, W], U8, name="scales_" + tag, tag="scales_" + tag, bufs=bufs, align_bytes=64)
            c0, c1 = (0, W) if half is None else (half * W // 2, (half + 1) * W // 2)
            nc.vector.quantize_mx(
                out=tiles[("codes",) + key][:, c0:c1].bitcast(fmt), scales=tiles[("scales",) + key][:, c0:c1],
                in_=src[:, c0 * PACK : c1 * PACK],
            )

        def quantise_tokens(gate, u):
            quantise(("tok", gate, u), tiles["tok", gate, u], E5M2, "tok", 9)

        def turn(gate, u, jjs=(0, 1)):
            words = tiles["tok", gate, u][:].bitcast(F32)
            for jj in jjs:
                tiles["turned", gate, u, jj] = bank(1 + jj, "turned")
                for t in range(PACK):
                    nc.tensor.transpose(
                        tiles["turned", gate, u, jj][:, t * P : (t + 1) * P],
                        words[:, 2 * P * t + jj : 2 * P * (t + 1) : 2], ident[:],
                    )

        def group_features(gate, u, jj, on_vector=False):
            if jj == 0:
                tiles["feat", gate, u] = work.tile([P, UNIT], BF16, name="feat", tag="feat", bufs=3, align_bytes=64)
            move = nc.vector.tensor_copy if on_vector else nc.scalar.copy
            move(
                out=tiles["feat", gate, u][:, jj * 2 * W : (jj + 1) * 2 * W].rearrange("q (e p t) -> q e p t", e=2, t=PACK),
                in_=tiles["turned", gate, u, jj][:].bitcast(BF16).rearrange("q (t p e) -> q e p t", e=2, t=PACK),
            )

        def group_both(gate, u):
            group_features(gate, u, 0)
            group_features(gate, u, 1)

        def quantise_features(gate, u, half=None):
            quantise(("feat", gate, u), tiles["feat", gate, u], E5M2, "feat", 3, half)

        def load_eng(g):
            tiles["eng_raw", g] = work.tile([P, UNIT], BF16, name="raw", tag="raw", bufs=3)
            nc.sync.dma_start(
                out=by_slot(tiles["eng_raw", g][:]),
                in_=eng_out[g * W : (g + 1) * W, :].rearrange("(p j) d -> p j d", j=PACK),
            )

        def group_eng(g):
            tiles["eng", g] = work.tile([P, UNIT], BF16, name="side", tag="side", bufs=2, align_bytes=64)
            nc.scalar.copy(
                out=tiles["eng", g][:].rearrange("p (c i j) -> p c j i", i=PACK, j=PACK),
                in_=tiles["eng_raw", g][:].rearrange("p (j c i) -> p c j i", i=PACK, j=PACK),
            )

        def quantise_eng(g):
            quantise(("eng", g), tiles["eng", g], E4M3, "eng", 2)

        def load_w(gate, c):
            tiles["w_raw", gate, c] = work.tile([P, UNIT], BF16, name="raw", tag="raw", bufs=3)
            col0 = gate * DHID + c * W
            nc.sync.dma_start(
                out=by_slot(tiles["w_raw", gate, c][:]),
                in_=w_ih[:DOUT, col0 : col0 + W].rearrange("(dt p) f -> p dt f", p=P),
            )

        def turn_w(gate, c):
            words = tiles["w_raw", gate, c][:].bitcast(F32)
            for pair in range(2):
                tiles["w_turned", gate, c, pair] = bank(1 + pair, "w_turned")
                for k in range(PACK):
                    dt = 2 * pair + k // 2
                    nc.tensor.transpose(
                        tiles["w_turned", gate, c, pair][:, k * P : (k + 1) * P],
                        words[:, 2 * P * dt + k % 2 : 2 * P * (dt + 1) : 2], ident[:],
                    )

        def group_w(gate, c, pairs=(0, 1)):
            if 0 in pairs:
                tiles["w", gate, c] = work.tile([P, UNIT], BF16, name="side", tag="side", bufs=2, align_bytes=64)
            for pair in pairs:
                nc.scalar.copy(
                    out=tiles["w", gate, c][:, pair * 2 * W : (pair + 1) * 2 * W].bitcast(F32).rearrange("q (d r v) -> q d r v", d=2, v=2),
                    in_=tiles["w_turned", gate, c, pair][:].rearrange("q (d v r) -> q d r v", d=2, v=2),
                )

        def quantise_w(gate, c):
            quantise(("w", gate, c), tiles["w", gate, c], E4M3, "w", 6)

        def staging(key):
            if key not in tiles:
                tiles[key] = work.tile([P, UNIT], F32, name="staging", tag="staging", bufs=3)
            return tiles[key]

        def weight_grad(gate, c, dt, b):
            acc = bank(b, "dw")
            tiles["dw", gate, c, dt] = acc
            for g in range(2):
                u = UNITS.index((c, g))
                nc.tensor.matmul_mx(
                    out=acc[:],
                    lhsT=tiles["codes", "eng", g][:, dt * P : (dt + 1) * P].bitcast(E4M3),
                    lhsT_scale=tiles["scales", "eng", g][:, dt * P : (dt + 1) * P],
                    rhs=tiles["codes", "tok", gate, u][:].bitcast(E5M2),
                    rhs_scale=tiles["scales", "tok", gate, u][:],
                    start=(g == 0), stop=(g == 1),
                )

        def empty_weight_grad(gate, c, dt, on_vector=False):
            dst = staging(("dw_out", gate, c))[:, dt * W : (dt + 1) * W].rearrange("p (m t) -> p m t", t=PACK)
            src = tiles["dw", gate, c, dt][:].rearrange("p (t m) -> p m t", t=PACK)
            if on_vector:
                nc.vector.tensor_copy(out=dst, in_=src)
            else:
                nc.scalar.copy(out=dst, in_=src)

        def store_weight_grad(gate, c, dts):
            col0 = gate * DHID + c * W
            nc.sync.dma_start(
                out=out_1[:DOUT, col0 : col0 + W].rearrange("(dt p) f -> p dt f", p=P)[:, dts, :],
                in_=by_slot(tiles["dw_out", gate, c][:])[:, dts, :],
            )

        def input_grad(g, j, gate, c, b=None):
            if b is not None:
                tiles["dx", g, j] = bank(b, "dx")
            u = UNITS.index((c, g))
            nc.tensor.matmul_mx(
                out=tiles["dx", g, j][:],
                lhsT=tiles["codes", "feat", gate, u][:, j * P : (j + 1) * P].bitcast(E5M2),
                lhsT_scale=tiles["scales", "feat", gate, u][:, j * P : (j + 1) * P],
                rhs=tiles["codes", "w", gate, c][:].bitcast(E4M3),
                rhs_scale=tiles["scales", "w", gate, c][:],
                start=(b is not None), stop=(gate == GATE_R and u != 1),
            )

        first_half = keep.tile([P, UNIT], F32, name="first_half")

        def park_input_grad(j):
            nc.scalar.copy(out=first_half[:, j * W : (j + 1) * W], in_=tiles["dx", 0, j][:])

        def empty_input_grad(g, j):
            dst = staging(("dx_out", g))[:, j * W : (j + 1) * W]
            if g == 0:
                nc.vector.tensor_tensor(out=dst, in0=tiles["dx", g, j][:], in1=first_half[:, j * W : (j + 1) * W], op=ALU.add)
            else:
                nc.scalar.copy(out=dst, in_=tiles["dx", g, j][:])

        def store_input_grad(g, js):
            nc.sync.dma_start(
                out=out_0[g * W : (g + 1) * W, :].rearrange("(p j) d -> p j d", j=PACK)[:, js, :],
                in_=by_slot(tiles["dx_out", g][:])[:, js, :],
            )

        def input_passes(gate, u, js=range(PACK)):
            c, g = UNITS[u]
            for j in js:
                input_grad(g, j, gate, c, 4 + j if (gate == GATE_N and u != 2) else None)

        waiting = []
        filled = []

        def next_dw(refill=True, b=3, on_vector=False):
            if filled:
                gate, c, dt = filled.pop()
                empty_weight_grad(gate, c, dt, on_vector)
                if dt == PACK - 1:
                    store_weight_grad(gate, c, slice(0, PACK))
            if refill and waiting:
                gate, c, dt = waiting.pop(0)
                weight_grad(gate, c, dt, b)
                filled.append((gate, c, dt))

        def queue_dw(gate, u):
            c, g = UNITS[u]
            if u % 2 == 1:
                waiting.extend([(gate, c, dt) for dt in range(PACK)])

        def w_pass(gate, c):
            turn_w(gate, c)
            group_w(gate, c)

        def round_shared(gate, u, split):
            round_tokens(gate, u, True, 0, split)
            round_tokens(gate, u, False, split, P)

        load("g", 0)
        load("n", 0, 0)
        load("h", 0, 0)
        load("z", 0, 0)
        load_eng(0)
        load("n", 0, 1)
        load("h", 0, 1)
        load("z", 0, 1)
        load_w(GATE_N, 0)
        load_tension()
        load("r", 0)
        load("g", 1)
        load_w(GATE_Z, 0)
        load("n", 1)
        load("h", 1)
        load("hn", 0)
        faction_sums(0)
        n_minus_h(0, 0)
        square_n(0, 0)
        pull_back(0, 0)
        pull_back(0, 1)
        group_eng(0)
        load_eng(1)
        through_z(0, 0)
        n_minus_h(0, 1)
        square_n(0, 1)
        through_z(0, 1)
        widen_tension()
        w_pass(GATE_N, 0)
        load_w(GATE_R, 0)
        load("z", 1)
        load("r", 1)
        load("hn", 1)
        finish_dn(0, 0)
        finish_dn(0, 1)

        for u in range(len(UNITS)):
            c, g = UNITS[u]
            last = u == len(UNITS) - 1
            if u > 0:
                through_z(u)
                if not last:
                    load("n", u + 1)
                    load("z", u + 1)
                last_row_sums(GATE_R, u - 1, range(2))
                round_tokens(GATE_R, u - 1, on_vector=(u in RVEC))
                next_dw()
                quantise_features(GATE_Z, u - 1)
                turn(GATE_R, u - 1)
                if u < 3:
                    square_r(u)
                finish_dn(u)
                queue_dw(GATE_Z, u - 1)
                next_dw()
                input_passes(GATE_Z, u - 1)
                if u == 2:
                    round_tokens(GATE_N, u)
                    next_dw()
                last_row_sums(GATE_R, u - 1, range(2, 3))
                group_features(GATE_R, u - 1, 0)
                next_dw()
                last_row_sums(GATE_R, u - 1, range(3, 4))
                group_features(GATE_R, u - 1, 1)
                if not last:
                    load("r", u + 1)
                if u == 1:
                    turn_w(GATE_R, 0)
            if last:
                break
            if u == 0:
                square_r(0)
            if u == 2:
                next_dw()
                turn(GATE_N, u)
                next_dw()
                faction_sums(u + 1)
            last_row_sums(GATE_N, u, range(2))
            if u < 2:
                round_tokens(GATE_N, u)
            if u == 1:
                group_w(GATE_R, 0)
                load_w(GATE_Z, 1)
                load_w(GATE_R, 1)
            if u < 2:
                faction_sums(u + 1)
            times_z(u)
            if u > 0:
                quantise_tokens(GATE_R, u - 1)
            else:
                quantise_w(GATE_N, 0)
                quantise_eng(0)
            if u < 2:
                turn(GATE_N, u)
            finish_dz(u)
            last_row_sums(GATE_N, u, range(2, 3))
            if u == 1:
                quantise_eng(1)
                quantise_w(GATE_R, 0)
            if u == 2:
                quantise_w(GATE_N, 1)
            if u > 0:
                quantise_features(GATE_R, u - 1)
                input_passes(GATE_R, u - 1)
            quantise_tokens(GATE_N, u)
            if u < 2:
                last_row_sums(GATE_N, u, range(3, 4))
            round_tokens(GATE_Z, u)
            group_features(GATE_N, u, 0)
            if u == 1:
                for j in range(PACK):
                    park_input_grad(j)
            group_features(GATE_N, u, 1)
            n_minus_h(u + 1)
            if u == 2:
                turn_w(GATE_Z, c)
                last_row_sums(GATE_N, u, range(3, 4))
            last_row_sums(GATE_Z, u, range(2))
            if u == 0:
                turn_w(GATE_Z, c)
            fold_slots(GATE_Z, u, [0])
            pull_back(u + 1)
            fold_slots(GATE_Z, u, [1])
            if u + 2 < len(UNITS):
                load("g", u + 2)
                load("h", u + 2)
            square_n(u + 1, 0)
            if u != 1:
                group_w(GATE_Z, c)
            if u == 0:
                load_w(GATE_N, 1)
            if u == 1:
                queue_dw(GATE_N, 1)
            if u == 2:
                queue_dw(GATE_R, 1)
            next_dw()
            turn(GATE_Z, u)
            times_hn(u)
            fold_slots(GATE_Z, u, [2])
            if u + 2 < len(UNITS):
                load("hn", u + 2)
            last_row_sums(GATE_Z, u, range(2, 3))
            square_n(u + 1, 1)
            next_dw()
            quantise_tokens(GATE_Z, u)
            quantise_features(GATE_N, u)
            fold_slots(GATE_Z, u, [3])
            if u != 1:
                quantise_w(GATE_Z, c)
            if u == 2:
                square_r(3, 0)
            input_passes(GATE_N, u)
            if u == 0:
                group_eng(1)
            group_features(GATE_Z, u, 0)
            next_dw()
            group_features(GATE_Z, u, 1)
            if u > 0:
                turn_w(GATE_N if u == 1 else GATE_R, 1)
                next_dw()
                group_w(GATE_N if u == 1 else GATE_R, 1)
            last_row_sums(GATE_Z, u, range(3, 4))
            folded_sums(GATE_Z, u)
            finish_dr(u)

        u = len(UNITS) - 1
        quantise_w(GATE_R, 1)
        square_r(u, 1)
        round_tokens(GATE_N, u)
        last_row_sums(GATE_N, u, range(1))
        times_z(u)
        quantise_tokens(GATE_R, u - 1)
        quantise_features(GATE_R, u - 1)
        input_passes(GATE_R, u - 1)
        turn(GATE_N, u)
        finish_dz(u)
        quantise_tokens(GATE_N, u)
        last_row_sums(GATE_N, u, range(1, 2))
        weight_grad(GATE_N, 1, 0, 3)
        for j in range(PACK):
            empty_input_grad(1, j)
        store_input_grad(1, slice(0, PACK))
        for dt in range(1, PACK):
            weight_grad(GATE_N, 1, dt, 3 + dt)
        last_row_sums(GATE_N, u, range(2, 3))
        group_both(GATE_N, u)
        round_tokens(GATE_Z, u, on_vector=True)
        turn(GATE_Z, u)
        last_row_sums(GATE_N, u, range(3, 4))
        fold_slots(GATE_Z, u, [0])
        times_hn(u)
        fold_slots(GATE_Z, u, [1])
        for dt in range(PACK):
            empty_weight_grad(GATE_N, 1, dt)
        store_weight_grad(GATE_N, 1, slice(0, PACK))
        last_row_sums(GATE_Z, u, range(2))
        quantise_tokens(GATE_Z, u)
        fold_slots(GATE_Z, u, [2])
        weight_grad(GATE_Z, 1, 0, 3)
        weight_grad(GATE_Z, 1, 1, 7)
        quantise_features(GATE_N, u)
        fold_slots(GATE_Z, u, [3])
        input_passes(GATE_N, u, range(3))
        group_both(GATE_Z, u)
        finish_dr(u)
        empty_weight_grad(GATE_Z, 1, 0)
        weight_grad(GATE_Z, 1, 2, 3)
        empty_weight_grad(GATE_Z, 1, 1)
        store_weight_grad(GATE_Z, 1, slice(0, 2))
        weight_grad(GATE_Z, 1, 3, 7)
        round_shared(GATE_R, u, TAIL_SPLIT)
        folded_sums(GATE_Z, u)
        turn(GATE_R, u)
        empty_weight_grad(GATE_Z, 1, 2)
        empty_weight_grad(GATE_Z, 1, 3)
        store_weight_grad(GATE_Z, 1, slice(2, 4))
        quantise_features(GATE_Z, u)
        quantise_tokens(GATE_R, u)
        input_passes(GATE_Z, u, range(2))
        fold_slots(GATE_R, u, [0])
        weight_grad(GATE_R, 1, 0, 3)
        group_features(GATE_R, u, 0)
        quantise_features(GATE_R, u, 0)
        input_passes(GATE_R, u, range(2))
        fold_slots(GATE_R, u, [1])
        group_features(GATE_R, u, 1)
        weight_grad(GATE_R, 1, 1, 1)
        input_passes(GATE_Z, u, range(2, 3))
        input_passes(GATE_N, u, range(3, 4))
        input_passes(GATE_Z, u, range(3, 4))
        empty_input_grad(0, 0)
        store_input_grad(0, slice(0, 1))
        fold_slots(GATE_R, u, [2])
        quantise_features(GATE_R, u, 1)
        empty_weight_grad(GATE_R, 1, 0)
        store_weight_grad(GATE_R, 1, slice(0, 1))
        weight_grad(GATE_R, 1, 2, 2)
        input_passes(GATE_R, u, range(2, 4))
        weight_grad(GATE_R, 1, 3, 3)
        fold_slots(GATE_R, u, [3])
        empty_weight_grad(GATE_R, 1, 1)
        store_weight_grad(GATE_R, 1, slice(1, 2))
        last_row_sums(GATE_Z, u, range(2, 4))
        last_row_sums(GATE_R, u)
        folded_sums(GATE_R, u)
        empty_input_grad(0, 1)
        store_input_grad(0, slice(1, 2))
        empty_weight_grad(GATE_R, 1, 2)
        store_weight_grad(GATE_R, 1, slice(2, 3))
        empty_input_grad(0, 2)
        store_input_grad(0, slice(2, 3))
        empty_weight_grad(GATE_R, 1, 3)
        store_weight_grad(GATE_R, 1, slice(3, 4))
        store_last_row()
        empty_input_grad(0, 3)
        store_input_grad(0, slice(3, 4))
